import numpy as np
import ml_dtypes


def mxq(x, axis, fmt="e4m3"):
    dtype, down = {"e4m3": (ml_dtypes.float8_e4m3fn, 7), "e5m2": (ml_dtypes.float8_e5m2, 14)}[fmt]
    v = np.moveaxis(np.asarray(x, np.float32).astype(ml_dtypes.bfloat16).astype(np.float64), axis, -1)
    blocks = v.reshape(v.shape[:-1] + (-1, 32))
    amax = np.abs(blocks).max(-1, keepdims=True)
    byte = np.maximum(np.where(amax > 0, np.frexp(amax)[1] - 1 + 127, 0) - down, 1)
    scale = np.exp2(byte - 127.0)
    codes = (blocks / scale).astype(np.float32).astype(dtype).astype(np.float64)
    return np.moveaxis((codes * scale).reshape(v.shape), -1, axis)


WIDE = False


def mx_kscale(k):
    if not WIDE:
        return np.ones(k)
    levels = np.array([10, -10, 5, -5, 0])
    if k % 512:
        return np.exp2(np.random.permutation(np.resize(levels, k // 32))).repeat(32)
    a = np.empty((k // 512, 16))
    for p in range(k // 512):
        a[p, :8] = np.random.permutation(np.resize(levels, 8))
        for g in range(8):
            far = levels[np.abs(levels - a[p, g]) >= 10]
            a[p, g + 8] = far[np.random.randint(len(far))]
    return np.exp2(a.ravel()).repeat(32)


BF16 = ml_dtypes.bfloat16


def bf(x):
    return np.asarray(x, np.float32).astype(BF16)


def f64(x):
    return np.asarray(x).astype(np.float64)


E2M1 = np.array([0.0, 0.5, 1.0, 1.5, 2.0, 3.0, 4.0, 6.0, -0.0, -0.5, -1.0, -1.5, -2.0, -3.0, -4.0, -6.0])


def pack_weight(w, fmt):
    k, n = w.shape
    w = f64(bf(w)).reshape(k // 32, 32, n)
    amax = np.abs(w).max(1)
    if fmt == "e4m3":
        byte = np.frexp(amax)[1] - 1 + 127 - 7
    else:
        mant, ex = np.frexp(amax / 6.0)
        byte = np.where(mant > 0.5, ex, ex - 1) + 127
    byte = np.clip(np.where(amax > 0, byte, 1), 1, 254)
    scaled = (w * np.exp2(127.0 - byte)[:, None, :]).reshape(k, n).astype(np.float32)
    by_word = np.ascontiguousarray(scaled.reshape(k // 512, 128, 4, n).transpose(0, 1, 3, 2))
    if fmt == "e4m3":
        words = by_word.astype(ml_dtypes.float8_e4m3fn).view(np.uint8)
    else:
        c = by_word.astype(ml_dtypes.float4_e2m1fn).view(np.uint8) & 0xF
        words = c[..., 0::2] | (c[..., 1::2] << 4)
    return np.ascontiguousarray(words), np.ascontiguousarray(byte.astype(np.uint8).reshape(k // 512, 16, n))


def unpack_weight(words, scales, fmt):
    g, p, n, _ = words.shape
    if fmt == "e4m3":
        vals = np.ascontiguousarray(words).view(ml_dtypes.float8_e4m3fn).astype(np.float64)
    else:
        nib = np.empty((g, p, n, 4), np.uint8)
        nib[..., 0::2] = words & 0xF
        nib[..., 1::2] = words >> 4
        vals = E2M1[nib]
    vals = vals * np.repeat(np.exp2(scales.astype(np.float64) - 127.0), 8, axis=1)[..., None]
    return vals.transpose(0, 1, 3, 2).reshape(g * 512, n)


B, IN, M, OUT = 1024, 1024, 512, 512
F = 2 * M
EPS = 1e-12


def draw0():
    s, t = mx_kscale(IN), mx_kscale(F)
    x = bf(np.random.standard_normal((B, IN)) * s)
    W1_words, W1_scales = pack_weight(np.random.standard_normal((IN, F)) / np.sqrt(IN) / s[:, None] * t, "e4m3")
    b1 = bf(np.random.standard_normal(F) * 0.1 * t)
    W2_words, W2_scales = pack_weight(np.random.standard_normal((F, M)) / np.sqrt(F) / t[:, None], "e4m3")
    b2 = bf(np.random.standard_normal(M) * 0.3)
    return {"x": x,
            "W1_words": W1_words, "W1_scales": W1_scales,
            "b1": b1,
            "W2_words": W2_words, "W2_scales": W2_scales,
            "b2": b2}


def core(x, W1_words, W1_scales, b1, W2_words, W2_scales, b2):
    h = np.maximum((mxq(f64(x), 1, "e4m3") @ unpack_weight(W1_words, W1_scales, "e4m3")) + f64(b1), 0.0)
    v = (mxq(h, 1, "e4m3") @ unpack_weight(W2_words, W2_scales, "e4m3")) + f64(b2)
    norm = np.sqrt(np.sum(v * v, axis=-1, keepdims=True))
    return v / np.maximum(norm, EPS)


def e4m3fn_bytes(y):
    return np.clip(np.asarray(y, np.float64), -448.0, 448.0).astype(np.float32).astype(ml_dtypes.float8_e4m3fn).view(np.uint8)


def e4m3fn_values(b):
    return np.asarray(b, np.uint8).view(ml_dtypes.float8_e4m3fn).astype(np.float64)


def setup_inputs():
    d = draw0()
    x0 = np.asarray(d['x']).astype(np.float64)
    s = (np.max(np.abs(x0), axis=(0,), keepdims=True) / 448.0).astype(np.float32)
    out = {}
    for k, v in d.items():
        if k == 'x':
            out['x_bytes'] = e4m3fn_bytes(x0 / s.astype(np.float64))
            out['x_scale'] = s
        else:
            out[k] = v
    return out


def reference(x_bytes, x_scale, W1_words, W1_scales, b1, W2_words, W2_scales, b2):
    return core(e4m3fn_values(x_bytes) * x_scale.astype(np.float64), W1_words, W1_scales, b1, W2_words, W2_scales, b2)

from contextlib import ExitStack

import concourse.mybir as mybir
from concourse.masks import make_identity

FLOPS = 2 * 1024 * 1024 * 1024 + 2 * 1024 * 1024 * 512

F32 = mybir.dt.float32
BF16 = mybir.dt.bfloat16
U32 = mybir.dt.uint32
I32 = mybir.dt.int32
U8 = mybir.dt.uint8
FP8 = mybir.dt.float8_e4m3fn
FP8X4 = mybir.dt.float8_e4m3fn_x4
ACT = mybir.ActivationFunctionType
ALU = mybir.AluOpType

P = 128
K = 1024
NOUT = 512
CHUNKS = ((0, 1), (128, 2), (384, 2), (640, 2), (896, 1))
S_WEAVE = ((0,0),(0,0),(0,0),(0,0),(0,0))
FIN = ("G", "GG", "GG", "GG", "V")
NCH = len(CHUNKS)


def tile_geometricmanifoldnetwork_pa_w8_kernel(
    tc, x_bytes, x_scale, W1_words, W1_scales, b1, W2_words, W2_scales, b2, out
):
    nc = tc.nc
    with ExitStack() as ctx:
        keep = ctx.enter_context(tc.tile_pool(name="keep", bufs=1))
        work = ctx.enter_context(tc.tile_pool(name="work", bufs=3))
        psx = ctx.enter_context(tc.psum_pool(name="psx", bufs=1))
        psh = ctx.enter_context(tc.psum_pool(name="psh", bufs=4))
        psy = ctx.enter_context(tc.psum_pool(name="psy", bufs=2))
        ctx.enter_context(tc.manual_schedule())

        s1raw = keep.tile([P, K], U8, name="s1raw", align_bytes=64)
        s1 = keep.tile([P, K], U8, name="s1", align_bytes=64)
        s2 = keep.tile([P, NOUT], U8, name="s2", align_bytes=64)
        nc.vector.memset(s1raw[:].bitcast(I32), 0)
        nc.vector.memset(s2[:].bitcast(I32), 0)
        half = keep.tile([P, 2], F32, name="half")
        nc.vector.memset(half[:], -0.5)
        warm = keep.tile([P, 2], BF16, name="warm")
        nc.scalar.activation(out=warm[:], in_=half[:], func=ACT.Relu)
        ident = keep.tile([P, P], F32, name="ident", align_bytes=64)
        make_identity(nc, ident[:])

        xbytes = []
        for c, (t0, J) in enumerate(CHUNKS):
            xbytes.append(keep.tile([P, J, K], U8, name="xbytes%d" % c, align_bytes=64))

        def load_x(c):
            t0, J = CHUNKS[c]
            nc.sync.dma_start(out=xbytes[c][:], in_=x_bytes[t0 : t0 + P * J, :].rearrange("(p j) k -> p j k", j=J))

        w1raw = [keep.tile([P, 2, 512], I32, name="w1raw%d" % t, align_bytes=64) for t in range(2)]
        w1 = [keep.tile([P, 2, 512], U32, name="w1_%d" % t, align_bytes=64) for t in range(2)]
        w2 = keep.tile([P, 2, 512], U32, name="w2", align_bytes=64)

        xsc = keep.tile([P, 2, 2, 2], F32, name="xsc")
        nc.scalar.dma_start(
            out=xsc[:].rearrange("p g u e -> p g (u e)"),
            in_=x_scale.rearrange("o (g p t) -> p (o g) t", g=2, t=4),
        )
        b1t = keep.tile([P, 2, 4], BF16, name="b1t")
        nc.scalar.dma_start(out=b1t[:], in_=b1.rearrange("(g p t) -> p g t", g=2, t=4))

        load_x(0)
        load_x(1)
        for q in range(4):
            nc.sync.dma_start(
                out=s1raw[32 * q : 32 * q + 8, :].bitcast(I32),
                in_=W1_scales[:, 4 * q : 4 * q + 4, :].bitcast(I32),
            )
        w1i = W1_words.rearrange("g p n t -> p g (n t)").bitcast(I32)
        for t in range(2):
            nc.sync.dma_start(out=w1raw[t][:], in_=w1i[:, :, 512 * t : 512 * t + 512])
        load_x(2)
        nc.sync.dma_start(out=w2[:].bitcast(I32), in_=W2_words.rearrange("g p n t -> p g (n t)").bitcast(I32))
        for q in range(4):
            nc.sync.dma_start(
                out=s2[32 * q : 32 * q + 8, :].bitcast(I32),
                in_=W2_scales[:, 4 * q : 4 * q + 4, :].bitcast(I32),
            )
        load_x(3)
        load_x(4)
        b2t = keep.tile([P, NOUT], BF16, name="b2t")
        nc.sync.dma_start(out=b2t[:], in_=b2.partition_broadcast(P))

        xv = [keep.tile([P, J, K], BF16, name="xv%d" % c, align_bytes=64) for c, (t0, J) in enumerate(CHUNKS)]
        xt = {}
        grp = {}
        xq = {}
        xs = {}
        ph = {}
        hp = {}
        hg = {}
        hq = {}
        hs = {}
        py = {}
        v = {}
        ssq = {}

        def cast(c, j):
            nc.scalar.copy(out=xv[c][:, j, :], in_=xbytes[c][:, j, :].bitcast(FP8))

        def turn(c):
            J = CHUNKS[c][1]
            for g in range(2):
                xt[c, g] = psx.tile([P, 2, P * J], F32, name="xt%d" % g)
            words = xv[c][:].bitcast(F32)
            for j in range(J):
                for g in range(2):
                    for u in range(2):
                        nc.tensor.transpose(
                            xt[c, g][:, u, P * j : P * j + P],
                            words[:, j, 256 * g + u : 256 * (g + 1) : 2],
                            ident[:],
                        )

        def scale_x(c, g):
            n = P * CHUNKS[c][1]
            if g == 0:
                grp[c] = work.tile([P, 2, n, 4], BF16, name="grp", align_bytes=64)
            nc.vector.tensor_tensor(
                out=grp[c][:, g, :, :].rearrange("p n (u e) -> p n u e", e=2),
                in0=xt[c, g][:].bitcast(BF16).rearrange("p u (n e) -> p n u e", e=2),
                in1=xsc[:, g, :, :].unsqueeze(1).to_broadcast([P, n, 2, 2]),
                op=ALU.mult,
            )

        def quant_x(c):
            n = P * CHUNKS[c][1]
            xq[c] = work.tile([P, 2, n], U32, name="xq", align_bytes=64)
            xs[c] = work.tile([P, 2, n], U8, name="xs", align_bytes=64)
            nc.vector.quantize_mx(
                out=xq[c][:].rearrange("p g n -> p (g n)").bitcast(FP8X4),
                scales=xs[c][:].rearrange("p g n -> p (g n)"),
                in_=grp[c][:].rearrange("p g n t -> p (g n t)"),
            )

        def stage1(c, T):
            n = P * CHUNKS[c][1]
            for t in range(4):
                if t % 2 == 0:
                    ph[c, T, t // 2] = psh.tile([P, 2, n], F32, name="ph")
                cols = slice(128 * t, 128 * t + 128)
                for g in range(2):
                    nc.tensor.matmul_mx(
                        out=ph[c, T, t // 2][:, t % 2, :],
                        lhsT=w1[T][:, g, cols].bitcast(FP8X4),
                        lhsT_scale=s1[4 * g :, 512 * T + 128 * t : 512 * T + 128 * t + 128],
                        rhs=xq[c][:, g, :].bitcast(FP8X4),
                        rhs_scale=xs[c][:, g, :],
                        start=(g == 0),
                        stop=(g == 1),
                    )

        def exit_h(c, T):
            n = P * CHUNKS[c][1]
            hp[c, T] = work.tile([P, 4, n], BF16, name="hp", align_bytes=64)
            for t in range(4):
                nc.scalar.activation(
                    out=hp[c, T][:, t, :],
                    in_=ph[c, T, t // 2][:, t % 2, :],
                    func=ACT.Relu,
                    bias=b1t[:, T, t : t + 1],
                )

        def weave_h(c, T):
            n = P * CHUNKS[c][1]
            hg[c, T] = work.tile([P, n, 4], BF16, name="hg", align_bytes=64)
            cut = n - S_WEAVE[c][T]
            for copy, cols in ((nc.vector.tensor_copy, slice(0, cut)), (nc.scalar.copy, slice(cut, n))):
                if cols.start < cols.stop:
                    copy(
                        out=hg[c, T][:, cols, :].rearrange("p (c i) t -> p c t i", i=4),
                        in_=hp[c, T][:, :, cols].rearrange("p t (c i) -> p c t i", i=4),
                    )

        def quant_h(c, T):
            n = P * CHUNKS[c][1]
            if T == 0:
                hq[c] = work.tile([P, 2, n], U32, name="hq", align_bytes=64)
                hs[c] = work.tile([P, 2, n], U8, name="hs", align_bytes=64)
            nc.vector.quantize_mx(
                out=hq[c][:, T, :].bitcast(FP8X4),
                scales=hs[c][:, T, :],
                in_=hg[c, T][:].rearrange("p n t -> p (n t)"),
            )

        def stage2(c):
            for j in range(CHUNKS[c][1]):
                py[c, j] = psy.tile([P, NOUT], F32, name="py")
                for T in range(2):
                    nc.tensor.matmul_mx(
                        out=py[c, j][:],
                        lhsT=hq[c][:, T, P * j : P * j + P].bitcast(FP8X4),
                        lhsT_scale=hs[c][:, T, P * j : P * j + P],
                        rhs=w2[:, T, :].bitcast(FP8X4),
                        rhs_scale=s2[4 * T :, :],
                        start=(T == 0),
                        stop=(T == 1),
                    )

        def bias_v(c, j):
            J = CHUNKS[c][1]
            if j == 0:
                v[c] = work.tile([P, J, NOUT], F32, name="v", align_bytes=64)
                ssq[c] = work.tile([P, 2], F32, name="ssq")
            nc.vector.tensor_tensor(out=v[c][:, j, :], in0=py[c, j][:], in1=b2t[:], op=ALU.add)

        def square_v(c, j):
            junk = work.tile([P, NOUT], BF16, name="junk", align_bytes=64)
            nc.scalar.activation(out=junk[:], in_=v[c][:, j, :], func=ACT.Square, accum_out=ssq[c][:, j : j + 1])

        def finish_v(c):
            t0, J = CHUNKS[c]
            clamped = work.tile([P, 2], F32, name="clamped")
            r = work.tile([P, 2], F32, name="r")
            o = work.tile([P, J, NOUT], F32, name="o", align_bytes=64)
            nc.gpsimd.tensor_scalar(
                out=clamped[:, 0:J], in0=ssq[c][:, 0:J], scalar1=1e-24, scalar2=None, op0=ALU.max
            )
            nc.gpsimd.tensor_tensor(out=r[:, 0:J], in0=clamped[:, 0:J], in1=half[:, 0:J], op=ALU.pow)
            for j in range(J):
                if FIN[c][j] == "S":
                    nc.scalar.activation(out=o[:, j, :], in_=v[c][:, j, :], func=ACT.Copy, scale=r[:, j : j + 1])
                elif FIN[c][j] == "V":
                    nc.vector.tensor_scalar(
                        out=o[:, j, :], in0=v[c][:, j, :], scalar1=r[:, j : j + 1], scalar2=None, op0=ALU.mult
                    )
                else:
                    nc.gpsimd.tensor_scalar(
                        out=o[:, j, :], in0=v[c][:, j, :], scalar1=r[:, j : j + 1], scalar2=0.0,
                        op0=ALU.mult, op1=ALU.add,
                    )
            nc.sync.dma_start(out=out[t0 : t0 + P * J, :].rearrange("(p j) o -> p j o", j=J), in_=o[:])

        def permute_w1(T):
            nc.vector.tensor_copy(
                out=w1[T][:].bitcast(I32).rearrange("p g (t m) -> p g m t", t=4),
                in_=w1raw[T][:].rearrange("p g (m t) -> p g m t", t=4),
            )

        def live(c):
            return 0 <= c < NCH

        nc.scalar.copy(out=xv[0][:, 0, 0:512], in_=xbytes[0][:, 0, 0:512].bitcast(FP8))
        nc.vector.tensor_copy(out=xv[0][:, 0, 512:1024], in_=xbytes[0][:, 0, 512:1024].bitcast(FP8))
        turn(0)
        cast(1, 0)
        nc.vector.tensor_copy(out=xv[1][:, 1, :], in_=xbytes[1][:, 1, :].bitcast(FP8))

        for s in range(NCH + 2):
            a, b, c = s, s - 1, s - 2
            if live(a):
                scale_x(a, 0)
                scale_x(a, 1)
            if s == 0:
                nc.vector.tensor_copy(
                    out=s1[:].rearrange("p (a t m) -> p a t m", a=2, t=4),
                    in_=s1raw[:].rearrange("p (a m t) -> p a t m", a=2, t=4),
                )
                permute_w1(0)
            if live(b):
                stage1(b, 0)
                exit_h(b, 0)
            if live(c):
                stage2(c)
            if live(a):
                quant_x(a)
            if live(b):
                weave_h(b, 0)
                stage1(b, 1)
                exit_h(b, 1)
            if live(c):
                for j in range(CHUNKS[c][1]):
                    bias_v(c, j)
                    square_v(c, j)
            if s == 0:
                permute_w1(1)
            if live(a + 2):
                for j in range(CHUNKS[a + 2][1]):
                    cast(a + 2, j)
            if live(a + 1):
                turn(a + 1)
            if live(b):
                weave_h(b, 1)
                quant_h(b, 0)
                quant_h(b, 1)
            if live(c):
                finish_v(c)
